import numpy as np
import ml_dtypes


def mxq(x, axis, fmt="e4m3"):
    dtype, down = {"e4m3": (ml_dtypes.float8_e4m3fn, 7), "e5m2": (ml_dtypes.float8_e5m2, 14)}[fmt]
    v = np.moveaxis(np.asarray(x, np.float32).astype(ml_dtypes.bfloat16).astype(np.float64), axis, -1)
    blocks = v.reshape(v.shape[:-1] + (-1, 32))
    amax = np.abs(blocks).max(-1, keepdims=True)
    byte = np.maximum(np.where(amax > 0, np.frexp(amax)[1] - 1 + 127, 0) - down, 1)
    scale = np.exp2(byte - 127.0)
    codes = (blocks / scale).astype(np.float32).astype(dtype).astype(np.float64)
    return np.moveaxis((codes * scale).reshape(v.shape), -1, axis)


BF16 = ml_dtypes.bfloat16


def bf(x):
    return np.asarray(x, np.float32).astype(BF16)


def f64(x):
    return np.asarray(x).astype(np.float64)


B, N, F = 4, 128, 16384

EMP = 0.1
EPS = 1e-8
ZERO = 9e-15


def setup_inputs():
    g = np.random.standard_normal((B, 1, F))
    a = (1.0 + 2.0 * np.random.random((B, N, 1))) * (2.0 * np.random.randint(0, 2, (B, N, 1)) - 1.0)
    x = np.random.standard_normal((B, N, F)) + a * g
    w = 1.0 + 0.5 * np.random.standard_normal((1, N, F))
    return {"x": bf(x), "w": bf(w)}


def reference(x, w):
    xw = f64(x) * f64(w)
    nrm = np.maximum(np.sqrt(np.sum(xw * xw, axis=-1, keepdims=True)), EPS)
    xn = xw / nrm
    xq = mxq(xn, 2, "e4m3")
    cos = xq @ xq.transpose(0, 2, 1)
    return np.where(cos > EMP, cos, ZERO)

@@ -1,0 +1,189 @@
+import concourse.masks as masks
+import concourse.mybir as mybir
+
+BF16 = mybir.dt.bfloat16
+F32 = mybir.dt.float32
+U32 = mybir.dt.uint32
+U8 = mybir.dt.uint8
+FP8X4 = mybir.dt.float8_e4m3fn_x4
+ALU = mybir.AluOpType
+ACT = mybir.ActivationFunctionType
+AXIS = mybir.AxisListType
+
+BATCH, NODES, FEATURES = 4, 128, 16384
+EMP = 0.1
+EPS = 1e-8
+ZERO = 9e-15
+
+P = 128
+PACK = 4
+GROUP_NODES = P // PACK
+GROUPS = NODES // GROUP_NODES
+ROW = FEATURES // PACK
+HALF = ROW // 2
+HALVES = ROW // HALF
+BANK_BLOCKS = 8
+BANK_COLS = BANK_BLOCKS * P
+HALF_BANKS = HALF // BANK_COLS
+ROUNDS = ROW // BANK_COLS
+TILES = BATCH * GROUPS
+AHEAD = 2
+
+FLOPS = 2 * BATCH * NODES * NODES * FEATURES
+
+
+def tile_simmetricblock_k_kernel(tc, x, w, out):
+    nc = tc.nc
+    x_tiles = x.rearrange("b (g n) (j c) -> (b g) (n j) c", g=GROUPS, j=PACK)
+    w_tiles = w.rearrange("o (g n) (j c) -> (o g) (n j) c", g=GROUPS, j=PACK)
+
+    with (
+        tc.tile_pool(name="const", bufs=1) as const,
+        tc.tile_pool(name="x_in", bufs=6) as x_in,
+        tc.tile_pool(name="products", bufs=6) as products,
+        tc.tile_pool(name="squares", bufs=2) as squares,
+        tc.tile_pool(name="norms", bufs=3) as norms,
+        tc.tile_pool(name="normed", bufs=4) as normed,
+        tc.tile_pool(name="grouped", bufs=2 * ROUNDS) as grouped_pool,
+        tc.tile_pool(name="packed", bufs=4) as packed,
+        tc.tile_pool(name="result", bufs=2) as result,
+        tc.psum_pool(name="turned", bufs=4) as turned_pool,
+        tc.psum_pool(name="totals", bufs=2) as totals,
+        tc.psum_pool(name="gram", bufs=2) as gram_pool,
+    ):
+        one = const.tile([P, 1], F32)
+        nc.vector.memset(one[:], 1.0)
+        warm = const.tile([P, 1], F32)
+        nc.scalar.activation(out=warm[:], in_=one[:], func=ACT.Sqrt)
+
+        identity = const.tile([P, P], BF16)
+        masks.make_identity(nc, identity[:])
+        node_of = const.tile([P, GROUP_NODES], F32)
+        nc.vector.tensor_reduce(
+            out=node_of[:],
+            in_=identity[:].rearrange("p (n j) -> p n j", j=PACK),
+            axis=AXIS.X,
+            op=ALU.add,
+        )
+        same_node = const.tile([P, GROUP_NODES, PACK], F32)
+        nc.vector.tensor_copy(
+            out=same_node[:], in_=node_of[:].unsqueeze(2).to_broadcast([P, GROUP_NODES, PACK])
+        )
+
+        w_halves = {}
+        x_halves = {}
+        xw_halves = {}
+        sums = {}
+        grouped = {}
+        gram = {}
+
+        def load(t):
+            g = t % GROUPS
+            for h in range(HALVES):
+                cols = slice(h * HALF, (h + 1) * HALF)
+                if t < GROUPS:
+                    w_halves[g, h] = const.tile([P, HALF], BF16, name="w_%d_%d" % (g, h))
+                    nc.sync.dma_start(out=w_halves[g, h][:], in_=w_tiles[g, :, cols])
+                x_halves[t, h] = x_in.tile([P, HALF], BF16, name="x_half")
+                nc.sync.dma_start(out=x_halves[t, h][:], in_=x_tiles[t, :, cols])
+
+        def multiply_and_square(t):
+            g = t % GROUPS
+            sums[t] = norms.tile([P, HALVES], F32, name="sum_sq")
+            for h in range(HALVES):
+                xw_halves[t, h] = products.tile([P, HALF], F32, name="xw_half")
+                nc.vector.tensor_tensor(
+                    out=xw_halves[t, h][:], in0=x_halves[t, h][:], in1=w_halves[g, h][:], op=ALU.mult
+                )
+                unused = squares.tile([P, HALF], BF16)
+                nc.scalar.activation(
+                    out=unused[:],
+                    in_=xw_halves[t, h][:],
+                    func=ACT.Square,
+                    accum_out=sums[t][:, h : h + 1],
+                )
+
+        def normalise_and_turn(t):
+            b, g = divmod(t, GROUPS)
+            total = totals.tile([P, 1], F32)
+            for h in range(HALVES):
+                nc.tensor.matmul(
+                    out=total[:],
+                    lhsT=same_node[:].rearrange("p n j -> p (n j)"),
+                    rhs=sums[t][:, h : h + 1],
+                    start=(h == 0),
+                    stop=(h == HALVES - 1),
+                )
+            norm = norms.tile([P, 1], F32)
+            nc.scalar.activation(out=norm[:], in_=total[:], func=ACT.Sqrt)
+            clamped = norms.tile([P, 1], F32)
+            nc.vector.tensor_scalar_max(out=clamped[:], in0=norm[:], scalar1=EPS)
+            inverse = norms.tile([P, 1], F32)
+            nc.vector.reciprocal(out=inverse[:], in_=clamped[:])
+
+            for h in range(HALVES):
+                xn_half = normed.tile([P, HALF], BF16)
+                nc.vector.tensor_scalar(
+                    out=xn_half[:],
+                    in0=xw_halves[t, h][:],
+                    scalar1=inverse[:, 0:1],
+                    scalar2=None,
+                    op0=ALU.mult,
+                )
+                for k in range(HALF_BANKS):
+                    r = h * HALF_BANKS + k
+                    if g == 0:
+                        grouped[b, r] = grouped_pool.tile(
+                            [P, BANK_BLOCKS, GROUPS, P], BF16, name="grouped_round", align_bytes=64
+                        )
+                    turned = turned_pool.tile([P, BANK_BLOCKS, P], BF16)
+                    for s in range(BANK_BLOCKS):
+                        c0 = k * BANK_COLS + s * P
+                        nc.tensor.transpose(turned[:, s, :], xn_half[:, c0 : c0 + P], identity[:])
+                    nc.scalar.copy(out=grouped[b, r][:, :, g, :], in_=turned[:])
+
+        def quantise_and_multiply(b):
+            gram[b] = gram_pool.tile([P, NODES], F32, name="gram_b")
+            for r in range(ROUNDS):
+                codes = packed.tile([P, BANK_BLOCKS * NODES], U32, align_bytes=64)
+                scales = packed.tile([P, BANK_BLOCKS * NODES], U8, align_bytes=64)
+                nc.vector.quantize_mx(
+                    out=codes[:].bitcast(FP8X4),
+                    scales=scales[:],
+                    in_=grouped[b, r][:].rearrange("p s g q -> p (s g q)"),
+                )
+                for s in range(BANK_BLOCKS):
+                    nodes = slice(s * NODES, (s + 1) * NODES)
+                    nc.tensor.matmul_mx(
+                        out=gram[b][:],
+                        lhsT=codes[:, nodes].bitcast(FP8X4),
+                        lhsT_scale=scales[:, nodes],
+                        rhs=codes[:, nodes].bitcast(FP8X4),
+                        rhs_scale=scales[:, nodes],
+                        start=(r == 0 and s == 0),
+                        stop=(r == ROUNDS - 1 and s == BANK_BLOCKS - 1),
+                    )
+
+        def threshold_and_store(b):
+            cos = result.tile([P, NODES], F32)
+            nc.scalar.copy(out=cos[:], in_=gram[b][:])
+            kept = result.tile([P, NODES], F32)
+            nc.vector.scalar_tensor_tensor(
+                out=kept[:], in0=cos[:], scalar=EMP, in1=cos[:], op0=ALU.is_gt, op1=ALU.mult
+            )
+            final = result.tile([P, NODES], F32)
+            nc.vector.tensor_scalar_max(out=final[:], in0=kept[:], scalar1=ZERO)
+            nc.sync.dma_start(out=out[b], in_=final[:])
+
+        for t in range(AHEAD):
+            load(t)
+        for t in range(TILES + 1):
+            if t + AHEAD < TILES:
+                load(t + AHEAD)
+            if t < TILES:
+                multiply_and_square(t)
+            if t >= 1:
+                normalise_and_turn(t - 1)
+                if t % GROUPS == 0:
+                    quantise_and_multiply(t // GROUPS - 1)
+                    threshold_and_store(t // GROUPS - 1)

@@ -20,44 +20,222 @@ PACK = 4
 GROUP_NODES = P // PACK
 GROUPS = NODES // GROUP_NODES
 ROW = FEATURES // PACK
-HALF = ROW // 2
-HALVES = ROW // HALF
-BANK_BLOCKS = 8
-BANK_COLS = BANK_BLOCKS * P
-HALF_BANKS = HALF // BANK_COLS
-ROUNDS = ROW // BANK_COLS
-TILES = BATCH * GROUPS
-AHEAD = 2
+CHUNK = 1024
+CHUNKS = ROW // CHUNK
+WORDS = CHUNK // 2
+BLOCKS = WORDS // P
+PASSES = 2 * BLOCKS
+PAIR = P // 2
+SLABS = BATCH * GROUPS
+W_AHEAD = 2
+DIRECT = 3
+PIECES = (4, 2, 2)
 
 FLOPS = 2 * BATCH * NODES * NODES * FEATURES
 
 
 def tile_simmetricblock_k_kernel(tc, x, w, out):
     nc = tc.nc
-    x_tiles = x.rearrange("b (g n) (j c) -> (b g) (n j) c", g=GROUPS, j=PACK)
-    w_tiles = w.rearrange("o (g n) (j c) -> (o g) (n j) c", g=GROUPS, j=PACK)
+    x_slabs = x.rearrange("b (g n) (j c) -> (b g) (n j) c", g=GROUPS, j=PACK)
+    w_slabs = w.rearrange("o (g n) (j c) -> (o g) (n j) c", g=GROUPS, j=PACK)
 
     with (
         tc.tile_pool(name="const", bufs=1) as const,
-        tc.tile_pool(name="x_in", bufs=6) as x_in,
-        tc.tile_pool(name="products", bufs=6) as products,
+        tc.tile_pool(name="x_in", bufs=3) as x_in,
+        tc.tile_pool(name="products", bufs=3) as products,
         tc.tile_pool(name="squares", bufs=2) as squares,
         tc.tile_pool(name="norms", bufs=3) as norms,
-        tc.tile_pool(name="normed", bufs=4) as normed,
-        tc.tile_pool(name="grouped", bufs=2 * ROUNDS) as grouped_pool,
-        tc.tile_pool(name="packed", bufs=4) as packed,
+        tc.tile_pool(name="normed", bufs=3) as normed,
+        tc.tile_pool(name="grouped", bufs=8) as grouped_pool,
+        tc.tile_pool(name="packed", bufs=3) as packed,
         tc.tile_pool(name="result", bufs=2) as result,
-        tc.psum_pool(name="turned", bufs=4) as turned_pool,
-        tc.psum_pool(name="totals", bufs=2) as totals,
-        tc.psum_pool(name="gram", bufs=2) as gram_pool,
+        tc.psum_pool(name="w_bank", bufs=3) as w_bank_pool,
+        tc.psum_pool(name="turned", bufs=3) as turned_pool,
+        tc.psum_pool(name="totals", bufs=1) as totals,
+        tc.psum_pool(name="gram", bufs=1) as gram_pool,
     ):
+        xs = {}
+        w_nat = {}
+        w_turned = {}
+        w_banks = {}
+        xw = {}
+        sums = {}
+        inverse = {}
+        xn = {}
+        grouped = {}
+        codes = {}
+        scales = {}
+        gram = {}
+        cosines = {}
+
+        def load(t):
+            pieces = PIECES[t] if t < len(PIECES) else 1
+            xs[t] = x_in.tile([P, ROW], BF16, name="x_slab")
+            if t < GROUPS:
+                w_nat[t] = grouped_pool.tile([P, ROW], BF16, name="grouped_chunk", align_bytes=64)
+            for k in range(pieces):
+                cols = slice(k * ROW // pieces, (k + 1) * ROW // pieces)
+                if t < GROUPS:
+                    nc.sync.dma_start(out=w_nat[t][:, cols], in_=w_slabs[t, :, cols])
+                nc.sync.dma_start(out=xs[t][:, cols], in_=x_slabs[t, :, cols])
+
+        def turn_w(g):
+            w_turned[g] = const.tile([P, CHUNKS, WORDS], F32, name="w_turned_%d" % g)
+            words = w_nat[g][:].bitcast(F32)
+            for r in range(CHUNKS):
+                turned = turned_pool.tile([P, BLOCKS, P], F32, name="turned")
+                for s in range(BLOCKS):
+                    c0 = r * WORDS + s * P
+                    nc.tensor.transpose(turned[:, s, :], words[:, c0 : c0 + P], identity[:])
+                source = turned[:].rearrange("p s q -> p (s q)")
+                if r % 2 == 0:
+                    nc.vector.tensor_copy(out=w_turned[g][:, r, :], in_=source)
+                else:
+                    nc.scalar.copy(out=w_turned[g][:, r, :], in_=source)
+
+        def spread_w(q):
+            t, r = divmod(q, CHUNKS)
+            if t < DIRECT or t >= SLABS:
+                return
+            g = t % GROUPS
+            w_banks[q] = w_bank_pool.tile([P, WORDS], F32, name="w_bank")
+            for s in range(BLOCKS):
+                cols = slice(s * P, (s + 1) * P)
+                nc.tensor.transpose(w_banks[q][:, cols], w_turned[g][:, r, cols], identity[:])
+
+        def multiply(t, r):
+            cols = slice(r * CHUNK, (r + 1) * CHUNK)
+            if r == 0:
+                xw[t] = products.tile([P, ROW], F32, name="xw_slab")
+            w_part = w_nat[t][:, cols] if t < DIRECT else w_banks[t * CHUNKS + r][:].bitcast(BF16)
+            nc.vector.tensor_tensor(out=xw[t][:, cols], in0=xs[t][:, cols], in1=w_part, op=ALU.mult)
+
+        def square(t, h):
+            if h == 0:
+                sums[t] = norms.tile([P, 2], F32, name="sum_sq")
+            half = ROW // 2
+            unused = squares.tile([P, half], BF16, name="unused")
+            nc.scalar.activation(
+                out=unused[:],
+                in_=xw[t][:, h * half : (h + 1) * half],
+                func=ACT.Square,
+                accum_out=sums[t][:, h : h + 1],
+            )
+
+        def root(t):
+            total = totals.tile([P, 1], F32, name="total")
+            for h in range(2):
+                nc.tensor.matmul(
+                    out=total[:],
+                    lhsT=same_node[:].rearrange("p n j -> p (n j)"),
+                    rhs=sums[t][:, h : h + 1],
+                    start=(h == 0),
+                    stop=(h == 1),
+                )
+            inverse[t] = norms.tile([P, 1], F32, name="norm")
+            nc.scalar.activation(out=inverse[t][:], in_=total[:], func=ACT.Sqrt)
+
+        def invert(t):
+            clamped = norms.tile([P, 1], F32, name="clamped")
+            nc.vector.tensor_scalar_max(out=clamped[:], in0=inverse[t][:], scalar1=EPS)
+            inverse[t] = norms.tile([P, 1], F32, name="inverse")
+            nc.vector.reciprocal(out=inverse[t][:], in_=clamped[:])
+
+        def normaliser(t, r):
+            if t == SLABS - 1:
+                return "vector" if r < 3 else "scalar"
+            if t == SLABS - 2 and r >= 2:
+                return "vector"
+            return "gpsimd"
+
+        def normalise(t, first=0, end=CHUNKS):
+            if first == 0:
+                xn[t] = normed.tile([P, ROW], BF16, name="xn_slab")
+            for r in range(first, end):
+                cols = slice(r * CHUNK, (r + 1) * CHUNK)
+                how = normaliser(t, r)
+                if how == "vector":
+                    nc.vector.tensor_scalar(
+                        out=xn[t][:, cols], in0=xw[t][:, cols], scalar1=inverse[t][:, 0:1], scalar2=None, op0=ALU.mult
+                    )
+                elif how == "scalar":
+                    nc.scalar.activation(
+                        out=xn[t][:, cols], in_=xw[t][:, cols], func=ACT.Copy, scale=inverse[t][:, 0:1]
+                    )
+                else:
+                    nc.gpsimd.tensor_scalar(
+                        out=xn[t][:, cols],
+                        in0=xw[t][:, cols],
+                        scalar1=inverse[t][:, 0:1],
+                        scalar2=0.0,
+                        op0=ALU.mult,
+                        op1=ALU.add,
+                    )
+
+        def on_vector(t, r):
+            return r == CHUNKS - 1 and t < SLABS - 2
+
+        def turn(t, r):
+            b, g = divmod(t, GROUPS)
+            if g == 0:
+                grouped[b, r] = grouped_pool.tile([P, PASSES, GROUPS, PAIR], F32, name="grouped_chunk", align_bytes=64)
+            words = xn[t][:].bitcast(F32)
+            turned = turned_pool.tile([P, BLOCKS, P], F32, name="turned")
+            for s in range(BLOCKS):
+                c0 = r * WORDS + s * P
+                nc.tensor.transpose(turned[:, s, :], words[:, c0 : c0 + P], pairing[:].rearrange("p h n j -> p (h n j)"))
+            source = turned[:].rearrange("p s (h q) -> p (s h) q", h=2)
+            if on_vector(t, r):
+                nc.vector.tensor_copy(out=grouped[b, r][:, :, g, :], in_=source)
+            else:
+                nc.scalar.copy(out=grouped[b, r][:, :, g, :], in_=source)
+
+        def quantise(b, r):
+            codes[b, r] = packed.tile([P, PASSES * NODES], U32, name="codes", align_bytes=64)
+            scales[b, r] = packed.tile([P, PASSES * NODES], U8, name="scales", align_bytes=64)
+            nc.vector.quantize_mx(
+                out=codes[b, r][:].bitcast(FP8X4),
+                scales=scales[b, r][:],
+                in_=grouped[b, r][:].rearrange("p a g q -> p (a g q)").bitcast(BF16),
+            )
+
+        def accumulate(b, r):
+            if r == 0:
+                gram[b] = gram_pool.tile([P, NODES], F32, name="gram_b")
+            for s in range(PASSES):
+                nodes = slice(s * NODES, (s + 1) * NODES)
+                nc.tensor.matmul_mx(
+                    out=gram[b][:],
+                    lhsT=codes[b, r][:, nodes].bitcast(FP8X4),
+                    lhsT_scale=scales[b, r][:, nodes],
+                    rhs=codes[b, r][:, nodes].bitcast(FP8X4),
+                    rhs_scale=scales[b, r][:, nodes],
+                    start=(r == 0 and s == 0),
+                    stop=(r == CHUNKS - 1 and s == PASSES - 1),
+                )
+
+        def fetch(b):
+            cosines[b] = result.tile([P, NODES], F32, name="cos")
+            nc.scalar.copy(out=cosines[b][:], in_=gram[b][:])
+
+        def threshold_and_store(b):
+            cos = cosines[b]
+            kept = result.tile([P, NODES], F32, name="kept")
+            nc.vector.scalar_tensor_tensor(
+                out=kept[:], in0=cos[:], scalar=EMP, in1=cos[:], op0=ALU.is_gt, op1=ALU.mult
+            )
+            final = result.tile([P, NODES], F32, name="final")
+            nc.vector.tensor_scalar_max(out=final[:], in0=kept[:], scalar1=ZERO)
+            nc.sync.dma_start(out=out[b], in_=final[:])
+
         one = const.tile([P, 1], F32)
         nc.vector.memset(one[:], 1.0)
         warm = const.tile([P, 1], F32)
         nc.scalar.activation(out=warm[:], in_=one[:], func=ACT.Sqrt)
-
-        identity = const.tile([P, P], BF16)
+        identity = const.tile([P, P], F32)
         masks.make_identity(nc, identity[:])
+        pairing = const.tile([P, 2, GROUP_NODES, 2], F32)
+        nc.vector.tensor_copy(out=pairing[:], in_=identity[:].rearrange("p (n h j) -> p h n j", h=2, j=2))
         node_of = const.tile([P, GROUP_NODES], F32)
         nc.vector.tensor_reduce(
             out=node_of[:],
@@ -70,120 +248,71 @@ def tile_simmetricblock_k_kernel(tc, x, w, out):
             out=same_node[:], in_=node_of[:].unsqueeze(2).to_broadcast([P, GROUP_NODES, PACK])
         )
 
-        w_halves = {}
-        x_halves = {}
-        xw_halves = {}
-        sums = {}
-        grouped = {}
-        gram = {}
-
-        def load(t):
-            g = t % GROUPS
-            for h in range(HALVES):
-                cols = slice(h * HALF, (h + 1) * HALF)
-                if t < GROUPS:
-                    w_halves[g, h] = const.tile([P, HALF], BF16, name="w_%d_%d" % (g, h))
-                    nc.sync.dma_start(out=w_halves[g, h][:], in_=w_tiles[g, :, cols])
-                x_halves[t, h] = x_in.tile([P, HALF], BF16, name="x_half")
-                nc.sync.dma_start(out=x_halves[t, h][:], in_=x_tiles[t, :, cols])
-
-        def multiply_and_square(t):
-            g = t % GROUPS
-            sums[t] = norms.tile([P, HALVES], F32, name="sum_sq")
-            for h in range(HALVES):
-                xw_halves[t, h] = products.tile([P, HALF], F32, name="xw_half")
-                nc.vector.tensor_tensor(
-                    out=xw_halves[t, h][:], in0=x_halves[t, h][:], in1=w_halves[g, h][:], op=ALU.mult
-                )
-                unused = squares.tile([P, HALF], BF16)
-                nc.scalar.activation(
-                    out=unused[:],
-                    in_=xw_halves[t, h][:],
-                    func=ACT.Square,
-                    accum_out=sums[t][:, h : h + 1],
-                )
-
-        def normalise_and_turn(t):
-            b, g = divmod(t, GROUPS)
-            total = totals.tile([P, 1], F32)
-            for h in range(HALVES):
-                nc.tensor.matmul(
-                    out=total[:],
-                    lhsT=same_node[:].rearrange("p n j -> p (n j)"),
-                    rhs=sums[t][:, h : h + 1],
-                    start=(h == 0),
-                    stop=(h == HALVES - 1),
-                )
-            norm = norms.tile([P, 1], F32)
-            nc.scalar.activation(out=norm[:], in_=total[:], func=ACT.Sqrt)
-            clamped = norms.tile([P, 1], F32)
-            nc.vector.tensor_scalar_max(out=clamped[:], in0=norm[:], scalar1=EPS)
-            inverse = norms.tile([P, 1], F32)
-            nc.vector.reciprocal(out=inverse[:], in_=clamped[:])
-
-            for h in range(HALVES):
-                xn_half = normed.tile([P, HALF], BF16)
-                nc.vector.tensor_scalar(
-                    out=xn_half[:],
-                    in0=xw_halves[t, h][:],
-                    scalar1=inverse[:, 0:1],
-                    scalar2=None,
-                    op0=ALU.mult,
-                )
-                for k in range(HALF_BANKS):
-                    r = h * HALF_BANKS + k
-                    if g == 0:
-                        grouped[b, r] = grouped_pool.tile(
-                            [P, BANK_BLOCKS, GROUPS, P], BF16, name="grouped_round", align_bytes=64
-                        )
-                    turned = turned_pool.tile([P, BANK_BLOCKS, P], BF16)
-                    for s in range(BANK_BLOCKS):
-                        c0 = k * BANK_COLS + s * P
-                        nc.tensor.transpose(turned[:, s, :], xn_half[:, c0 : c0 + P], identity[:])
-                    nc.scalar.copy(out=grouped[b, r][:, :, g, :], in_=turned[:])
-
-        def quantise_and_multiply(b):
-            gram[b] = gram_pool.tile([P, NODES], F32, name="gram_b")
-            for r in range(ROUNDS):
-                codes = packed.tile([P, BANK_BLOCKS * NODES], U32, align_bytes=64)
-                scales = packed.tile([P, BANK_BLOCKS * NODES], U8, align_bytes=64)
-                nc.vector.quantize_mx(
-                    out=codes[:].bitcast(FP8X4),
-                    scales=scales[:],
-                    in_=grouped[b, r][:].rearrange("p s g q -> p (s g q)"),
-                )
-                for s in range(BANK_BLOCKS):
-                    nodes = slice(s * NODES, (s + 1) * NODES)
-                    nc.tensor.matmul_mx(
-                        out=gram[b][:],
-                        lhsT=codes[:, nodes].bitcast(FP8X4),
-                        lhsT_scale=scales[:, nodes],
-                        rhs=codes[:, nodes].bitcast(FP8X4),
-                        rhs_scale=scales[:, nodes],
-                        start=(r == 0 and s == 0),
-                        stop=(r == ROUNDS - 1 and s == BANK_BLOCKS - 1),
-                    )
-
-        def threshold_and_store(b):
-            cos = result.tile([P, NODES], F32)
-            nc.scalar.copy(out=cos[:], in_=gram[b][:])
-            kept = result.tile([P, NODES], F32)
-            nc.vector.scalar_tensor_tensor(
-                out=kept[:], in0=cos[:], scalar=EMP, in1=cos[:], op0=ALU.is_gt, op1=ALU.mult
-            )
-            final = result.tile([P, NODES], F32)
-            nc.vector.tensor_scalar_max(out=final[:], in0=kept[:], scalar1=ZERO)
-            nc.sync.dma_start(out=out[b], in_=final[:])
-
-        for t in range(AHEAD):
-            load(t)
-        for t in range(TILES + 1):
-            if t + AHEAD < TILES:
-                load(t + AHEAD)
-            if t < TILES:
-                multiply_and_square(t)
-            if t >= 1:
-                normalise_and_turn(t - 1)
-                if t % GROUPS == 0:
-                    quantise_and_multiply(t // GROUPS - 1)
-                    threshold_and_store(t // GROUPS - 1)
+        with tc.manual_schedule():
+            load(0)
+            load(1)
+            for t in range(SLABS):
+                if t + 2 < SLABS:
+                    load(t + 2)
+                lag = t - 2
+                b, due = divmod(lag, GROUPS)
+                if lag >= 0:
+                    turn(lag, 0)
+                if lag >= 2 * GROUPS and due == 0:
+                    fetch(b - 2)
+                spread_w(t * CHUNKS + 2)
+                multiply(t, 0)
+                if lag >= 0:
+                    turn(lag, 1)
+                spread_w(t * CHUNKS + 3)
+                multiply(t, 1)
+                if lag >= GROUPS:
+                    quantise(b - 1, due)
+                if lag >= 2 * GROUPS and due == 0:
+                    threshold_and_store(b - 2)
+                if t >= 1:
+                    root(t - 1)
+                    invert(t - 1)
+                    normalise(t - 1, 0, CHUNKS if t < SLABS - 1 else 2)
+                square(t, 0)
+                if t == 2:
+                    turn_w(3)
+                if t == 3:
+                    turn_w(0)
+                if t == 4:
+                    turn_w(1)
+                if t == 5:
+                    turn_w(2)
+                spread_w(t * CHUNKS + 4)
+                multiply(t, 2)
+                if lag >= 0:
+                    turn(lag, 2)
+                if lag >= GROUPS:
+                    accumulate(b - 1, due)
+                spread_w(t * CHUNKS + 5)
+                multiply(t, 3)
+                if lag >= 0:
+                    turn(lag, 3)
+                square(t, 1)
+            last = SLABS - 1
+            normalise(last - 1, 2)
+            turn(last - 1, 0)
+            turn(last - 1, 1)
+            quantise(BATCH - 2, 2)
+            accumulate(BATCH - 2, 2)
+            quantise(BATCH - 2, 3)
+            root(last)
+            invert(last)
+            normalise(last)
+            turn(last - 1, 2)
+            turn(last - 1, 3)
+            accumulate(BATCH - 2, 3)
+            for r in range(CHUNKS):
+                turn(last, r)
+            fetch(BATCH - 2)
+            for r in range(CHUNKS):
+                quantise(BATCH - 1, r)
+                accumulate(BATCH - 1, r)
+            threshold_and_store(BATCH - 2)
+            fetch(BATCH - 1)
+            threshold_and_store(BATCH - 1)

@@ -154,6 +154,10 @@ def tile_simmetricblock_k_kernel(tc, x, w, out):
             for r in range(first, end):
                 cols = slice(r * CHUNK, (r + 1) * CHUNK)
                 how = normaliser(t, r)
+                if how == "gpsimd":
+                    if r % 2 == 1:
+                        continue
+                    cols = slice(r * CHUNK, (r + 2) * CHUNK)
                 if how == "vector":
                     nc.vector.tensor_scalar(
                         out=xn[t][:, cols], in0=xw[t][:, cols], scalar1=inverse[t][:, 0:1], scalar2=None, op0=ALU.mult

@@ -28,7 +28,8 @@ PASSES = 2 * BLOCKS
 PAIR = P // 2
 SLABS = BATCH * GROUPS
 W_AHEAD = 2
-DIRECT = 3
+DIRECT = 1
+SHARE = 512
 PIECES = (4, 2, 2)
 
 FLOPS = 2 * BATCH * NODES * NODES * FEATURES
@@ -73,25 +74,30 @@ def tile_simmetricblock_k_kernel(tc, x, w, out):
             xs[t] = x_in.tile([P, ROW], BF16, name="x_slab")
             if t < GROUPS:
                 w_nat[t] = grouped_pool.tile([P, ROW], BF16, name="grouped_chunk", align_bytes=64)
-            for k in range(pieces):
-                cols = slice(k * ROW // pieces, (k + 1) * ROW // pieces)
+            parts = [slice(k * ROW // pieces, (k + 1) * ROW // pieces) for k in range(pieces)]
+            for k, cols in enumerate(parts):
                 if t < GROUPS:
                     nc.sync.dma_start(out=w_nat[t][:, cols], in_=w_slabs[t, :, cols])
-                nc.sync.dma_start(out=xs[t][:, cols], in_=x_slabs[t, :, cols])
+                if t == 0:
+                    nc.sync.dma_start(out=xs[t][:, cols], in_=x_slabs[t, :, cols])
+            if t > 0:
+                for k, cols in enumerate(parts):
+                    nc.sync.dma_start(out=xs[t][:, cols], in_=x_slabs[t, :, cols])
 
-        def turn_w(g):
-            w_turned[g] = const.tile([P, CHUNKS, WORDS], F32, name="w_turned_%d" % g)
+        def turn_w(g, on_scalar, chunks=range(CHUNKS)):
+            if 0 in chunks:
+                w_turned[g] = const.tile([P, CHUNKS, WORDS], F32, name="w_turned_%d" % g)
             words = w_nat[g][:].bitcast(F32)
-            for r in range(CHUNKS):
+            for r in chunks:
                 turned = turned_pool.tile([P, BLOCKS, P], F32, name="turned")
                 for s in range(BLOCKS):
                     c0 = r * WORDS + s * P
                     nc.tensor.transpose(turned[:, s, :], words[:, c0 : c0 + P], identity[:])
                 source = turned[:].rearrange("p s q -> p (s q)")
-                if r % 2 == 0:
-                    nc.vector.tensor_copy(out=w_turned[g][:, r, :], in_=source)
-                else:
+                if r in on_scalar:
                     nc.scalar.copy(out=w_turned[g][:, r, :], in_=source)
+                else:
+                    nc.vector.tensor_copy(out=w_turned[g][:, r, :], in_=source)
 
         def spread_w(q):
             t, r = divmod(q, CHUNKS)
@@ -110,27 +116,36 @@ def tile_simmetricblock_k_kernel(tc, x, w, out):
             w_part = w_nat[t][:, cols] if t < DIRECT else w_banks[t * CHUNKS + r][:].bitcast(BF16)
             nc.vector.tensor_tensor(out=xw[t][:, cols], in0=xs[t][:, cols], in1=w_part, op=ALU.mult)
 
-        def square(t, h):
-            if h == 0:
-                sums[t] = norms.tile([P, 2], F32, name="sum_sq")
-            half = ROW // 2
-            unused = squares.tile([P, half], BF16, name="unused")
-            nc.scalar.activation(
-                out=unused[:],
-                in_=xw[t][:, h * half : (h + 1) * half],
-                func=ACT.Square,
-                accum_out=sums[t][:, h : h + 1],
-            )
+        def square(t, first, end, engine="scalar"):
+            if first == 0:
+                sums[t] = []
+            cols = slice(first * CHUNK, end * CHUNK)
+            part = norms.tile([P, 1], F32, name="sum_%d" % len(sums[t]))
+            sums[t].append(part)
+            if engine == "scalar":
+                unused = squares.tile([P, ROW // 2], BF16, name="unused")
+                nc.scalar.activation(
+                    out=unused[:, : (end - first) * CHUNK],
+                    in_=xw[t][:, cols],
+                    func=ACT.Square,
+                    accum_out=part[:],
+                )
+            else:
+                unused = squares.tile([P, CHUNK], BF16, name="unused_v")
+                nc.vector.scalar_tensor_tensor(
+                    out=unused[:], in0=xw[t][:, cols], scalar=1.0, in1=xw[t][:, cols], op0=ALU.mult, op1=ALU.mult,
+                    accum_out=part[:],
+                )
 
         def root(t):
             total = totals.tile([P, 1], F32, name="total")
-            for h in range(2):
+            for k, part in enumerate(sums[t]):
                 nc.tensor.matmul(
                     out=total[:],
                     lhsT=same_node[:].rearrange("p n j -> p (n j)"),
-                    rhs=sums[t][:, h : h + 1],
-                    start=(h == 0),
-                    stop=(h == 1),
+                    rhs=part[:],
+                    start=(k == 0),
+                    stop=(k == len(sums[t]) - 1),
                 )
             inverse[t] = norms.tile([P, 1], F32, name="norm")
             nc.scalar.activation(out=inverse[t][:], in_=total[:], func=ACT.Sqrt)
@@ -157,7 +172,10 @@ def tile_simmetricblock_k_kernel(tc, x, w, out):
                 if how == "gpsimd":
                     if r % 2 == 1:
                         continue
-                    cols = slice(r * CHUNK, (r + 2) * CHUNK)
+                    stop = (r + 2) * CHUNK
+                    if stop == ROW:
+                        stop -= SHARE
+                    cols = slice(r * CHUNK, stop)
                 if how == "vector":
                     nc.vector.tensor_scalar(
                         out=xn[t][:, cols], in0=xw[t][:, cols], scalar1=inverse[t][:, 0:1], scalar2=None, op0=ALU.mult
@@ -177,7 +195,13 @@ def tile_simmetricblock_k_kernel(tc, x, w, out):
                     )
 
         def on_vector(t, r):
-            return r == CHUNKS - 1 and t < SLABS - 2
+            return (r == CHUNKS - 1) and t < SLABS - 2
+
+        def scalar_share(t):
+            if SHARE:
+                nc.scalar.activation(
+                    out=xn[t][:, ROW - SHARE :], in_=xw[t][:, ROW - SHARE :], func=ACT.Copy, scale=inverse[t][:, 0:1]
+                )
 
         def turn(t, r):
             b, g = divmod(t, GROUPS)
@@ -260,15 +284,22 @@ def tile_simmetricblock_k_kernel(tc, x, w, out):
                     load(t + 2)
                 lag = t - 2
                 b, due = divmod(lag, GROUPS)
+                fresh = t + 1 < GROUPS
+                final = t == SLABS - 1
                 if lag >= 0:
                     turn(lag, 0)
                 if lag >= 2 * GROUPS and due == 0:
                     fetch(b - 2)
-                spread_w(t * CHUNKS + 2)
+                if t >= GROUPS - 1:
+                    spread_w(t * CHUNKS + 2)
                 multiply(t, 0)
                 if lag >= 0:
                     turn(lag, 1)
-                spread_w(t * CHUNKS + 3)
+                if t >= GROUPS - 1:
+                    spread_w(t * CHUNKS + 3)
+                elif t >= 1:
+                    spread_w(t * CHUNKS + 2)
+                    spread_w(t * CHUNKS + 3)
                 multiply(t, 1)
                 if lag >= GROUPS:
                     quantise(b - 1, due)
@@ -277,42 +308,50 @@ def tile_simmetricblock_k_kernel(tc, x, w, out):
                 if t >= 1:
                     root(t - 1)
                     invert(t - 1)
-                    normalise(t - 1, 0, CHUNKS if t < SLABS - 1 else 2)
-                square(t, 0)
-                if t == 2:
-                    turn_w(3)
-                if t == 3:
-                    turn_w(0)
-                if t == 4:
-                    turn_w(1)
-                if t == 5:
-                    turn_w(2)
-                spread_w(t * CHUNKS + 4)
+                    normalise(t - 1, 0, CHUNKS if not final else 2)
+                square(t, 0, 2)
+                if 1 <= t <= SLABS - 2:
+                    scalar_share(t - 1)
+                if t == GROUPS - 1:
+                    turn_w(0, (3,))
+                if not fresh:
+                    spread_w(t * CHUNKS + 4)
                 multiply(t, 2)
-                if lag >= 0:
+                if lag >= 0 and not final:
                     turn(lag, 2)
-                if lag >= GROUPS:
+                if lag >= GROUPS and not final:
                     accumulate(b - 1, due)
-                spread_w(t * CHUNKS + 5)
+                if not fresh:
+                    spread_w(t * CHUNKS + 5)
                 multiply(t, 3)
-                if lag >= 0:
+                if lag >= 0 and not final:
                     turn(lag, 3)
-                square(t, 1)
+                if not final:
+                    square(t, 2, 4)
+                if fresh:
+                    turn_w(t + 1, () if t == 0 else (3,) if t == 1 else (3,))
+                    spread_w(t * CHUNKS + 4)
+                    spread_w(t * CHUNKS + 5)
             last = SLABS - 1
+            square(last, 2, 3)
+            square(last, 3, 4, "vector")
             normalise(last - 1, 2)
+            turn(last - 2, 2)
+            turn(last - 2, 3)
+            accumulate(BATCH - 2, 1)
             turn(last - 1, 0)
-            turn(last - 1, 1)
-            quantise(BATCH - 2, 2)
-            accumulate(BATCH - 2, 2)
-            quantise(BATCH - 2, 3)
             root(last)
             invert(last)
             normalise(last)
+            turn(last - 1, 1)
+            quantise(BATCH - 2, 2)
+            quantise(BATCH - 2, 3)
             turn(last - 1, 2)
             turn(last - 1, 3)
-            accumulate(BATCH - 2, 3)
             for r in range(CHUNKS):
                 turn(last, r)
+            accumulate(BATCH - 2, 2)
+            accumulate(BATCH - 2, 3)
             fetch(BATCH - 2)
             for r in range(CHUNKS):
                 quantise(BATCH - 1, r)

@@ -147,14 +147,10 @@ def tile_simmetricblock_k_kernel(tc, x, w, out):
                     start=(k == 0),
                     stop=(k == len(sums[t]) - 1),
                 )
-            inverse[t] = norms.tile([P, 1], F32, name="norm")
-            nc.scalar.activation(out=inverse[t][:], in_=total[:], func=ACT.Sqrt)
-
-        def invert(t):
-            clamped = norms.tile([P, 1], F32, name="clamped")
-            nc.vector.tensor_scalar_max(out=clamped[:], in0=inverse[t][:], scalar1=EPS)
+            above = norms.tile([P, 1], F32, name="above")
+            nc.scalar.activation(out=above[:], in_=total[:], func=ACT.Relu, bias=minus_floor[:])
             inverse[t] = norms.tile([P, 1], F32, name="inverse")
-            nc.vector.reciprocal(out=inverse[t][:], in_=clamped[:])
+            nc.scalar.activation(out=inverse[t][:], in_=above[:], func=ACT.Abs_reciprocal_sqrt, bias=floor[:])
 
         def normaliser(t, r):
             if t == SLABS - 1:
@@ -195,7 +191,7 @@ def tile_simmetricblock_k_kernel(tc, x, w, out):
                     )
 
         def on_vector(t, r):
-            return (r == CHUNKS - 1) and t < SLABS - 2
+            return (r == CHUNKS - 1 or (r == 2 and t % 2 == 0)) and t < SLABS - 2
 
         def scalar_share(t):
             if SHARE:
@@ -259,7 +255,11 @@ def tile_simmetricblock_k_kernel(tc, x, w, out):
         one = const.tile([P, 1], F32)
         nc.vector.memset(one[:], 1.0)
         warm = const.tile([P, 1], F32)
-        nc.scalar.activation(out=warm[:], in_=one[:], func=ACT.Sqrt)
+        nc.scalar.activation(out=warm[:], in_=one[:], func=ACT.Abs_reciprocal_sqrt)
+        floor = const.tile([P, 1], F32)
+        nc.vector.tensor_scalar(out=floor[:], in0=one[:], scalar1=EPS * EPS, scalar2=None, op0=ALU.mult)
+        minus_floor = const.tile([P, 1], F32)
+        nc.vector.tensor_scalar(out=minus_floor[:], in0=one[:], scalar1=-EPS * EPS, scalar2=None, op0=ALU.mult)
         identity = const.tile([P, P], F32)
         masks.make_identity(nc, identity[:])
         pairing = const.tile([P, 2, GROUP_NODES, 2], F32)
@@ -286,6 +286,8 @@ def tile_simmetricblock_k_kernel(tc, x, w, out):
                 b, due = divmod(lag, GROUPS)
                 fresh = t + 1 < GROUPS
                 final = t == SLABS - 1
+                if t == 1:
+                    root(0)
                 if lag >= 0:
                     turn(lag, 0)
                 if lag >= 2 * GROUPS and due == 0:
@@ -305,15 +307,15 @@ def tile_simmetricblock_k_kernel(tc, x, w, out):
                     quantise(b - 1, due)
                 if lag >= 2 * GROUPS and due == 0:
                     threshold_and_store(b - 2)
-                if t >= 1:
+                if t >= 2:
                     root(t - 1)
-                    invert(t - 1)
+                if t >= 1:
                     normalise(t - 1, 0, CHUNKS if not final else 2)
                 square(t, 0, 2)
                 if 1 <= t <= SLABS - 2:
                     scalar_share(t - 1)
                 if t == GROUPS - 1:
-                    turn_w(0, (3,))
+                    turn_w(0, (1, 3))
                 if not fresh:
                     spread_w(t * CHUNKS + 4)
                 multiply(t, 2)
@@ -329,7 +331,7 @@ def tile_simmetricblock_k_kernel(tc, x, w, out):
                 if not final:
                     square(t, 2, 4)
                 if fresh:
-                    turn_w(t + 1, () if t == 0 else (3,) if t == 1 else (3,))
+                    turn_w(t + 1, () if t == 0 else (3,))
                     spread_w(t * CHUNKS + 4)
                     spread_w(t * CHUNKS + 5)
             last = SLABS - 1
@@ -341,7 +343,6 @@ def tile_simmetricblock_k_kernel(tc, x, w, out):
             accumulate(BATCH - 2, 1)
             turn(last - 1, 0)
             root(last)
-            invert(last)
             normalise(last)
             turn(last - 1, 1)
             quantise(BATCH - 2, 2)

@@ -29,7 +29,7 @@ PAIR = P // 2
 SLABS = BATCH * GROUPS
 W_AHEAD = 2
 DIRECT = 1
-SHARE = 512
+SHARE = 256
 PIECES = (4, 2, 2)
 
 FLOPS = 2 * BATCH * NODES * NODES * FEATURES
@@ -191,7 +191,7 @@ def tile_simmetricblock_k_kernel(tc, x, w, out):
                     )
 
         def on_vector(t, r):
-            return (r == CHUNKS - 1 or (r == 2 and t % 2 == 0)) and t < SLABS - 2
+            return (r == 3 or (r == 2 and t % 2 == 0 and t < 16)) and t < SLABS - 2
 
         def scalar_share(t):
             if SHARE:
@@ -311,11 +311,15 @@ def tile_simmetricblock_k_kernel(tc, x, w, out):
                     root(t - 1)
                 if t >= 1:
                     normalise(t - 1, 0, CHUNKS if not final else 2)
-                square(t, 0, 2)
+                if t == 0:
+                    square(t, 0, 1)
+                    square(t, 1, 2)
+                else:
+                    square(t, 0, 2)
                 if 1 <= t <= SLABS - 2:
                     scalar_share(t - 1)
                 if t == GROUPS - 1:
-                    turn_w(0, (1, 3))
+                    turn_w(0, (3,))
                 if not fresh:
                     spread_w(t * CHUNKS + 4)
                 multiply(t, 2)
@@ -331,7 +335,7 @@ def tile_simmetricblock_k_kernel(tc, x, w, out):
                 if not final:
                     square(t, 2, 4)
                 if fresh:
-                    turn_w(t + 1, () if t == 0 else (3,))
+                    turn_w(t + 1, ((2, 3), (3,), (3,))[t])
                     spread_w(t * CHUNKS + 4)
                     spread_w(t * CHUNKS + 5)
             last = SLABS - 1

@@ -29,7 +29,7 @@ PAIR = P // 2
 SLABS = BATCH * GROUPS
 W_AHEAD = 2
 DIRECT = 1
-SHARE = 256
+SHARE = 384
 PIECES = (4, 2, 2)
 
 FLOPS = 2 * BATCH * NODES * NODES * FEATURES
@@ -62,6 +62,7 @@ def tile_simmetricblock_k_kernel(tc, x, w, out):
         xw = {}
         sums = {}
         inverse = {}
+        raised = {}
         xn = {}
         grouped = {}
         codes = {}
@@ -147,10 +148,16 @@ def tile_simmetricblock_k_kernel(tc, x, w, out):
                     start=(k == 0),
                     stop=(k == len(sums[t]) - 1),
                 )
+            raised[t] = total
+
+        def rectify(t):
             above = norms.tile([P, 1], F32, name="above")
-            nc.scalar.activation(out=above[:], in_=total[:], func=ACT.Relu, bias=minus_floor[:])
+            nc.scalar.activation(out=above[:], in_=raised[t][:], func=ACT.Relu, bias=minus_floor[:])
+            raised[t] = above
+
+        def invert(t):
             inverse[t] = norms.tile([P, 1], F32, name="inverse")
-            nc.scalar.activation(out=inverse[t][:], in_=above[:], func=ACT.Abs_reciprocal_sqrt, bias=floor[:])
+            nc.scalar.activation(out=inverse[t][:], in_=raised[t][:], func=ACT.Abs_reciprocal_sqrt, bias=floor[:])
 
         def normaliser(t, r):
             if t == SLABS - 1:
@@ -191,7 +198,7 @@ def tile_simmetricblock_k_kernel(tc, x, w, out):
                     )
 
         def on_vector(t, r):
-            return (r == 3 or (r == 2 and t % 2 == 0 and t < 16)) and t < SLABS - 2
+            return (r == 3 or (r == 2 and t % 3 == 0)) and t < SLABS - 2
 
         def scalar_share(t):
             if SHARE:
@@ -292,32 +299,32 @@ def tile_simmetricblock_k_kernel(tc, x, w, out):
                     turn(lag, 0)
                 if lag >= 2 * GROUPS and due == 0:
                     fetch(b - 2)
-                if t >= GROUPS - 1:
+                if not fresh or t >= 1:
                     spread_w(t * CHUNKS + 2)
                 multiply(t, 0)
                 if lag >= 0:
                     turn(lag, 1)
-                if t >= GROUPS - 1:
-                    spread_w(t * CHUNKS + 3)
-                elif t >= 1:
-                    spread_w(t * CHUNKS + 2)
+                if t >= 2:
+                    root(t - 1)
+                if not fresh or t >= 1:
                     spread_w(t * CHUNKS + 3)
                 multiply(t, 1)
                 if lag >= GROUPS:
                     quantise(b - 1, due)
                 if lag >= 2 * GROUPS and due == 0:
                     threshold_and_store(b - 2)
-                if t >= 2:
-                    root(t - 1)
                 if t >= 1:
+                    rectify(t - 1)
+                if t >= 2:
+                    scalar_share(t - 2)
+                if t >= 1:
+                    invert(t - 1)
                     normalise(t - 1, 0, CHUNKS if not final else 2)
                 if t == 0:
                     square(t, 0, 1)
                     square(t, 1, 2)
                 else:
                     square(t, 0, 2)
-                if 1 <= t <= SLABS - 2:
-                    scalar_share(t - 1)
                 if t == GROUPS - 1:
                     turn_w(0, (3,))
                 if not fresh:
@@ -325,13 +332,13 @@ def tile_simmetricblock_k_kernel(tc, x, w, out):
                 multiply(t, 2)
                 if lag >= 0 and not final:
                     turn(lag, 2)
-                if lag >= GROUPS and not final:
-                    accumulate(b - 1, due)
                 if not fresh:
                     spread_w(t * CHUNKS + 5)
                 multiply(t, 3)
                 if lag >= 0 and not final:
                     turn(lag, 3)
+                if lag >= GROUPS and not final:
+                    accumulate(b - 1, due)
                 if not final:
                     square(t, 2, 4)
                 if fresh:
@@ -347,6 +354,8 @@ def tile_simmetricblock_k_kernel(tc, x, w, out):
             accumulate(BATCH - 2, 1)
             turn(last - 1, 0)
             root(last)
+            rectify(last)
+            invert(last)
             normalise(last)
             turn(last - 1, 1)
             quantise(BATCH - 2, 2)

@@ -29,6 +29,7 @@ PAIR = P // 2
 SLABS = BATCH * GROUPS
 W_AHEAD = 2
 DIRECT = 1
+LATE_W = {3: (0, 1), 4: (2, 3)}
 SHARE = 384
 PIECES = (4, 2, 2)
 
@@ -70,9 +71,15 @@ def tile_simmetricblock_k_kernel(tc, x, w, out):
         gram = {}
         cosines = {}
 
+        def place(t):
+            b, k = divmod(t, GROUPS)
+            return b, k if b % 2 == 0 else GROUPS - 1 - k
+
         def load(t):
             pieces = PIECES[t] if t < len(PIECES) else 1
             xs[t] = x_in.tile([P, ROW], BF16, name="x_slab")
+            b, g = place(t)
+            slab = b * GROUPS + g
             if t < GROUPS:
                 w_nat[t] = grouped_pool.tile([P, ROW], BF16, name="grouped_chunk", align_bytes=64)
             parts = [slice(k * ROW // pieces, (k + 1) * ROW // pieces) for k in range(pieces)]
@@ -80,13 +87,13 @@ def tile_simmetricblock_k_kernel(tc, x, w, out):
                 if t < GROUPS:
                     nc.sync.dma_start(out=w_nat[t][:, cols], in_=w_slabs[t, :, cols])
                 if t == 0:
-                    nc.sync.dma_start(out=xs[t][:, cols], in_=x_slabs[t, :, cols])
+                    nc.sync.dma_start(out=xs[t][:, cols], in_=x_slabs[slab, :, cols])
             if t > 0:
                 for k, cols in enumerate(parts):
-                    nc.sync.dma_start(out=xs[t][:, cols], in_=x_slabs[t, :, cols])
+                    nc.sync.dma_start(out=xs[t][:, cols], in_=x_slabs[slab, :, cols])
 
         def turn_w(g, on_scalar, chunks=range(CHUNKS)):
-            if 0 in chunks:
+            if chunks[0] == 0:
                 w_turned[g] = const.tile([P, CHUNKS, WORDS], F32, name="w_turned_%d" % g)
             words = w_nat[g][:].bitcast(F32)
             for r in chunks:
@@ -104,7 +111,7 @@ def tile_simmetricblock_k_kernel(tc, x, w, out):
             t, r = divmod(q, CHUNKS)
             if t < DIRECT or t >= SLABS:
                 return
-            g = t % GROUPS
+            g = place(t)[1]
             w_banks[q] = w_bank_pool.tile([P, WORDS], F32, name="w_bank")
             for s in range(BLOCKS):
                 cols = slice(s * P, (s + 1) * P)
@@ -207,8 +214,8 @@ def tile_simmetricblock_k_kernel(tc, x, w, out):
                 )
 
         def turn(t, r):
-            b, g = divmod(t, GROUPS)
-            if g == 0:
+            b, g = place(t)
+            if t % GROUPS == 0:
                 grouped[b, r] = grouped_pool.tile([P, PASSES, GROUPS, PAIR], F32, name="grouped_chunk", align_bytes=64)
             words = xn[t][:].bitcast(F32)
             turned = turned_pool.tile([P, BLOCKS, P], F32, name="turned")
@@ -325,18 +332,18 @@ def tile_simmetricblock_k_kernel(tc, x, w, out):
                     square(t, 1, 2)
                 else:
                     square(t, 0, 2)
-                if t == GROUPS - 1:
-                    turn_w(0, (3,))
-                if not fresh:
-                    spread_w(t * CHUNKS + 4)
+                if t in LATE_W:
+                    turn_w(0, (1, 3), LATE_W[t])
                 multiply(t, 2)
                 if lag >= 0 and not final:
                     turn(lag, 2)
                 if not fresh:
-                    spread_w(t * CHUNKS + 5)
+                    spread_w(t * CHUNKS + 4)
                 multiply(t, 3)
                 if lag >= 0 and not final:
                     turn(lag, 3)
+                if not fresh:
+                    spread_w(t * CHUNKS + 5)
                 if lag >= GROUPS and not final:
                     accumulate(b - 1, due)
                 if not final:

@@ -168,7 +168,7 @@ def tile_simmetricblock_k_kernel(tc, x, w, out):
 
         def normaliser(t, r):
             if t == SLABS - 1:
-                return "vector" if r < 3 else "scalar"
+                return "vector"
             if t == SLABS - 2 and r >= 2:
                 return "vector"
             return "gpsimd"
@@ -228,22 +228,27 @@ def tile_simmetricblock_k_kernel(tc, x, w, out):
             else:
                 nc.scalar.copy(out=grouped[b, r][:, :, g, :], in_=source)
 
-        def quantise(b, r):
-            codes[b, r] = packed.tile([P, PASSES * NODES], U32, name="codes", align_bytes=64)
-            scales[b, r] = packed.tile([P, PASSES * NODES], U8, name="scales", align_bytes=64)
+        def quantise(b, r, first=0, end=PASSES):
+            if first == 0:
+                codes[b, r] = packed.tile([P, PASSES * NODES], U32, name="codes", align_bytes=64)
+                scales[b, r] = packed.tile([P, PASSES * NODES], U8, name="scales", align_bytes=64)
+            cols = slice(first * NODES, end * NODES)
             nc.vector.quantize_mx(
-                out=codes[b, r][:].bitcast(FP8X4),
-                scales=scales[b, r][:],
-                in_=grouped[b, r][:].rearrange("p a g q -> p (a g q)").bitcast(BF16),
+                out=codes[b, r][:, cols].bitcast(FP8X4),
+                scales=scales[b, r][:, cols],
+                in_=grouped[b, r][:, first:end].rearrange("p a g q -> p (a g q)").bitcast(BF16),
             )
 
-        def accumulate(b, r):
-            if r == 0:
-                gram[b] = gram_pool.tile([P, NODES], F32, name="gram_b")
-            for s in range(PASSES):
+        def accumulate(b, r, first=0, end=PASSES):
+            if r == 0 and first == 0:
+                if b == BATCH - 1:
+                    gram[b] = w_bank_pool.tile([P, WORDS], F32, name="w_bank")
+                else:
+                    gram[b] = gram_pool.tile([P, WORDS], F32, name="gram_b")
+            for s in range(first, end):
                 nodes = slice(s * NODES, (s + 1) * NODES)
                 nc.tensor.matmul_mx(
-                    out=gram[b][:],
+                    out=gram[b][:, :NODES],
                     lhsT=codes[b, r][:, nodes].bitcast(FP8X4),
                     lhsT_scale=scales[b, r][:, nodes],
                     rhs=codes[b, r][:, nodes].bitcast(FP8X4),
@@ -254,7 +259,7 @@ def tile_simmetricblock_k_kernel(tc, x, w, out):
 
         def fetch(b):
             cosines[b] = result.tile([P, NODES], F32, name="cos")
-            nc.scalar.copy(out=cosines[b][:], in_=gram[b][:])
+            nc.scalar.copy(out=cosines[b][:], in_=gram[b][:, :NODES])
 
         def threshold_and_store(b):
             cos = cosines[b]
@@ -354,18 +359,18 @@ def tile_simmetricblock_k_kernel(tc, x, w, out):
                     spread_w(t * CHUNKS + 5)
             last = SLABS - 1
             square(last, 2, 3)
-            square(last, 3, 4, "vector")
+            square(last, 3, 4)
             normalise(last - 1, 2)
             turn(last - 2, 2)
             turn(last - 2, 3)
             accumulate(BATCH - 2, 1)
             turn(last - 1, 0)
+            quantise(BATCH - 2, 2)
             root(last)
             rectify(last)
             invert(last)
             normalise(last)
             turn(last - 1, 1)
-            quantise(BATCH - 2, 2)
             quantise(BATCH - 2, 3)
             turn(last - 1, 2)
             turn(last - 1, 3)
@@ -375,8 +380,11 @@ def tile_simmetricblock_k_kernel(tc, x, w, out):
             accumulate(BATCH - 2, 3)
             fetch(BATCH - 2)
             for r in range(CHUNKS):
-                quantise(BATCH - 1, r)
-                accumulate(BATCH - 1, r)
+                pieces = 2 if r == CHUNKS - 1 else 1
+                for k in range(pieces):
+                    span = (k * PASSES // pieces, (k + 1) * PASSES // pieces)
+                    quantise(BATCH - 1, r, *span)
+                    accumulate(BATCH - 1, r, *span)
             threshold_and_store(BATCH - 2)
             fetch(BATCH - 1)
             threshold_and_store(BATCH - 1)

@@ -29,9 +29,8 @@ PAIR = P // 2
 SLABS = BATCH * GROUPS
 W_AHEAD = 2
 DIRECT = 1
-LATE_W = {3: (0, 1), 4: (2, 3)}
 SHARE = 384
-PIECES = (4, 2, 2)
+PIECES = (4, 4, 2)
 
 FLOPS = 2 * BATCH * NODES * NODES * FEATURES
 
@@ -337,14 +336,14 @@ def tile_simmetricblock_k_kernel(tc, x, w, out):
                     square(t, 1, 2)
                 else:
                     square(t, 0, 2)
-                if t in LATE_W:
-                    turn_w(0, (1, 3), LATE_W[t])
                 multiply(t, 2)
                 if lag >= 0 and not final:
                     turn(lag, 2)
                 if not fresh:
                     spread_w(t * CHUNKS + 4)
                 multiply(t, 3)
+                if 0 <= t - GROUPS + 1 < CHUNKS:
+                    turn_w(0, (), (t - GROUPS + 1,))
                 if lag >= 0 and not final:
                     turn(lag, 3)
                 if not fresh:
@@ -354,9 +353,11 @@ def tile_simmetricblock_k_kernel(tc, x, w, out):
                 if not final:
                     square(t, 2, 4)
                 if fresh:
-                    turn_w(t + 1, ((2, 3), (3,), (3,))[t])
+                    turn_w(t + 1, ((3,), (3,), (3,))[t], (0,))
+                    turn_w(t + 1, ((3,), (3,), (3,))[t], (1, 2))
                     spread_w(t * CHUNKS + 4)
                     spread_w(t * CHUNKS + 5)
+                    turn_w(t + 1, ((3,), (3,), (3,))[t], (3,))
             last = SLABS - 1
             square(last, 2, 3)
             square(last, 3, 4)

@@ -29,7 +29,7 @@ PAIR = P // 2
 SLABS = BATCH * GROUPS
 W_AHEAD = 2
 DIRECT = 1
-SHARE = 384
+SHARE = 448
 PIECES = (4, 4, 2)
 
 FLOPS = 2 * BATCH * NODES * NODES * FEATURES
@@ -304,14 +304,14 @@ def tile_simmetricblock_k_kernel(tc, x, w, out):
                 b, due = divmod(lag, GROUPS)
                 fresh = t + 1 < GROUPS
                 final = t == SLABS - 1
+                if not fresh or t >= 1:
+                    spread_w(t * CHUNKS + 2)
                 if t == 1:
                     root(0)
                 if lag >= 0:
                     turn(lag, 0)
                 if lag >= 2 * GROUPS and due == 0:
                     fetch(b - 2)
-                if not fresh or t >= 1:
-                    spread_w(t * CHUNKS + 2)
                 multiply(t, 0)
                 if lag >= 0:
                     turn(lag, 1)
@@ -337,11 +337,11 @@ def tile_simmetricblock_k_kernel(tc, x, w, out):
                 else:
                     square(t, 0, 2)
                 multiply(t, 2)
-                if lag >= 0 and not final:
-                    turn(lag, 2)
                 if not fresh:
                     spread_w(t * CHUNKS + 4)
                 multiply(t, 3)
+                if lag >= 0 and not final:
+                    turn(lag, 2)
                 if 0 <= t - GROUPS + 1 < CHUNKS:
                     turn_w(0, (), (t - GROUPS + 1,))
                 if lag >= 0 and not final:
@@ -353,11 +353,11 @@ def tile_simmetricblock_k_kernel(tc, x, w, out):
                 if not final:
                     square(t, 2, 4)
                 if fresh:
-                    turn_w(t + 1, ((3,), (3,), (3,))[t], (0,))
-                    turn_w(t + 1, ((3,), (3,), (3,))[t], (1, 2))
+                    turn_w(t + 1, (3,), (0,))
+                    turn_w(t + 1, (3,), (1, 2))
                     spread_w(t * CHUNKS + 4)
                     spread_w(t * CHUNKS + 5)
-                    turn_w(t + 1, ((3,), (3,), (3,))[t], (3,))
+                    turn_w(t + 1, (3,), (3,))
             last = SLABS - 1
             square(last, 2, 3)
             square(last, 3, 4)

@@ -29,7 +29,7 @@ PAIR = P // 2
 SLABS = BATCH * GROUPS
 W_AHEAD = 2
 DIRECT = 1
-SHARE = 448
+SHARE = 0
 PIECES = (4, 4, 2)
 
 FLOPS = 2 * BATCH * NODES * NODES * FEATURES
@@ -204,7 +204,7 @@ def tile_simmetricblock_k_kernel(tc, x, w, out):
                     )
 
         def on_vector(t, r):
-            return (r == 3 or (r == 2 and t % 3 == 0)) and t < SLABS - 2
+            return r == 3 and t < SLABS - 2
 
         def scalar_share(t):
             if SHARE:

@@ -91,20 +91,21 @@ def tile_simmetricblock_k_kernel(tc, x, w, out):
                 for k, cols in enumerate(parts):
                     nc.sync.dma_start(out=xs[t][:, cols], in_=x_slabs[slab, :, cols])
 
-        def turn_w(g, on_scalar, chunks=range(CHUNKS)):
-            if chunks[0] == 0:
+        def turn_w(g, r, engine, spare):
+            if g not in w_turned:
                 w_turned[g] = const.tile([P, CHUNKS, WORDS], F32, name="w_turned_%d" % g)
             words = w_nat[g][:].bitcast(F32)
-            for r in chunks:
-                turned = turned_pool.tile([P, BLOCKS, P], F32, name="turned")
-                for s in range(BLOCKS):
-                    c0 = r * WORDS + s * P
-                    nc.tensor.transpose(turned[:, s, :], words[:, c0 : c0 + P], identity[:])
-                source = turned[:].rearrange("p s q -> p (s q)")
-                if r in on_scalar:
-                    nc.scalar.copy(out=w_turned[g][:, r, :], in_=source)
-                else:
-                    nc.vector.tensor_copy(out=w_turned[g][:, r, :], in_=source)
+            if spare:
+                bank = gram_pool.tile([P, WORDS], F32, name="gram_b")
+            else:
+                bank = turned_pool.tile([P, WORDS], F32, name="turned")
+            for s in range(BLOCKS):
+                c0 = r * WORDS + s * P
+                nc.tensor.transpose(bank[:, s * P : (s + 1) * P], words[:, c0 : c0 + P], identity[:])
+            if engine == "scalar":
+                nc.scalar.copy(out=w_turned[g][:, r, :], in_=bank[:])
+            else:
+                nc.vector.tensor_copy(out=w_turned[g][:, r, :], in_=bank[:])
 
         def spread_w(q):
             t, r = divmod(q, CHUNKS)
@@ -343,7 +344,7 @@ def tile_simmetricblock_k_kernel(tc, x, w, out):
                 if lag >= 0 and not final:
                     turn(lag, 2)
                 if 0 <= t - GROUPS + 1 < CHUNKS:
-                    turn_w(0, (), (t - GROUPS + 1,))
+                    turn_w(0, t - GROUPS + 1, "vector", False)
                 if lag >= 0 and not final:
                     turn(lag, 3)
                 if not fresh:
@@ -352,12 +353,20 @@ def tile_simmetricblock_k_kernel(tc, x, w, out):
                     accumulate(b - 1, due)
                 if not final:
                     square(t, 2, 4)
-                if fresh:
-                    turn_w(t + 1, (3,), (0,))
-                    turn_w(t + 1, (3,), (1, 2))
+                if t == 0:
+                    turn_w(1, 0, "vector", True)
+                    turn_w(1, 1, "vector", False)
+                    turn_w(1, 2, "vector", False)
+                    spread_w(4)
+                    spread_w(5)
+                    turn_w(1, 3, "scalar", False)
+                elif fresh:
+                    turn_w(t + 1, 0, "vector", False)
+                    turn_w(t + 1, 1, "vector", True)
+                    turn_w(t + 1, 2, "vector", False)
                     spread_w(t * CHUNKS + 4)
                     spread_w(t * CHUNKS + 5)
-                    turn_w(t + 1, (3,), (3,))
+                    turn_w(t + 1, 3, "scalar", False)
             last = SLABS - 1
             square(last, 2, 3)
             square(last, 3, 4)

import concourse.masks as masks
import concourse.mybir as mybir

BF16 = mybir.dt.bfloat16
F32 = mybir.dt.float32
U32 = mybir.dt.uint32
U8 = mybir.dt.uint8
FP8X4 = mybir.dt.float8_e4m3fn_x4
ALU = mybir.AluOpType
ACT = mybir.ActivationFunctionType
AXIS = mybir.AxisListType

BATCH, NODES, FEATURES = 4, 128, 16384
EMP = 0.1
EPS = 1e-8
ZERO = 9e-15

P = 128
PACK = 4
GROUP_NODES = P // PACK
GROUPS = NODES // GROUP_NODES
ROW = FEATURES // PACK
CHUNK = 1024
CHUNKS = ROW // CHUNK
WORDS = CHUNK // 2
BLOCKS = WORDS // P
PASSES = 2 * BLOCKS
PAIR = P // 2
SLABS = BATCH * GROUPS
W_AHEAD = 2
DIRECT = 1
SHARE = 0
PIECES = (4, 4, 2)

FLOPS = 2 * BATCH * NODES * NODES * FEATURES


def tile_simmetricblock_k_kernel(tc, x, w, out):
    nc = tc.nc
    x_slabs = x.rearrange("b (g n) (j c) -> (b g) (n j) c", g=GROUPS, j=PACK)
    w_slabs = w.rearrange("o (g n) (j c) -> (o g) (n j) c", g=GROUPS, j=PACK)

    with (
        tc.tile_pool(name="const", bufs=1) as const,
        tc.tile_pool(name="x_in", bufs=3) as x_in,
        tc.tile_pool(name="products", bufs=3) as products,
        tc.tile_pool(name="squares", bufs=2) as squares,
        tc.tile_pool(name="norms", bufs=3) as norms,
        tc.tile_pool(name="normed", bufs=3) as normed,
        tc.tile_pool(name="grouped", bufs=8) as grouped_pool,
        tc.tile_pool(name="packed", bufs=3) as packed,
        tc.tile_pool(name="result", bufs=2) as result,
        tc.psum_pool(name="w_bank", bufs=3) as w_bank_pool,
        tc.psum_pool(name="turned", bufs=3) as turned_pool,
        tc.psum_pool(name="totals", bufs=1) as totals,
        tc.psum_pool(name="gram", bufs=1) as gram_pool,
    ):
        xs = {}
        w_nat = {}
        w_turned = {}
        w_banks = {}
        xw = {}
        sums = {}
        inverse = {}
        raised = {}
        xn = {}
        grouped = {}
        codes = {}
        scales = {}
        gram = {}
        cosines = {}

        def place(t):
            b, k = divmod(t, GROUPS)
            return b, k if b % 2 == 0 else GROUPS - 1 - k

        def load(t):
            pieces = PIECES[t] if t < len(PIECES) else 1
            xs[t] = x_in.tile([P, ROW], BF16, name="x_slab")
            b, g = place(t)
            slab = b * GROUPS + g
            if t < GROUPS:
                w_nat[t] = grouped_pool.tile([P, ROW], BF16, name="grouped_chunk", align_bytes=64)
            parts = [slice(k * ROW // pieces, (k + 1) * ROW // pieces) for k in range(pieces)]
            for k, cols in enumerate(parts):
                if t < GROUPS:
                    nc.sync.dma_start(out=w_nat[t][:, cols], in_=w_slabs[t, :, cols])
                if t == 0:
                    nc.sync.dma_start(out=xs[t][:, cols], in_=x_slabs[slab, :, cols])
            if t > 0:
                for k, cols in enumerate(parts):
                    nc.sync.dma_start(out=xs[t][:, cols], in_=x_slabs[slab, :, cols])

        def turn_w(g, r, engine, spare):
            if g not in w_turned:
                w_turned[g] = const.tile([P, CHUNKS, WORDS], F32, name="w_turned_%d" % g)
            words = w_nat[g][:].bitcast(F32)
            if spare:
                bank = gram_pool.tile([P, WORDS], F32, name="gram_b")
            else:
                bank = turned_pool.tile([P, WORDS], F32, name="turned")
            for s in range(BLOCKS):
                c0 = r * WORDS + s * P
                nc.tensor.transpose(bank[:, s * P : (s + 1) * P], words[:, c0 : c0 + P], identity[:])
            if engine == "scalar":
                nc.scalar.copy(out=w_turned[g][:, r, :], in_=bank[:])
            else:
                nc.vector.tensor_copy(out=w_turned[g][:, r, :], in_=bank[:])

        def spread_w(q):
            t, r = divmod(q, CHUNKS)
            if t < DIRECT or t >= SLABS:
                return
            g = place(t)[1]
            w_banks[q] = w_bank_pool.tile([P, WORDS], F32, name="w_bank")
            for s in range(BLOCKS):
                cols = slice(s * P, (s + 1) * P)
                nc.tensor.transpose(w_banks[q][:, cols], w_turned[g][:, r, cols], identity[:])

        def multiply(t, r):
            cols = slice(r * CHUNK, (r + 1) * CHUNK)
            if r == 0:
                xw[t] = products.tile([P, ROW], F32, name="xw_slab")
            w_part = w_nat[t][:, cols] if t < DIRECT else w_banks[t * CHUNKS + r][:].bitcast(BF16)
            nc.vector.tensor_tensor(out=xw[t][:, cols], in0=xs[t][:, cols], in1=w_part, op=ALU.mult)

        def square(t, first, end, engine="scalar"):
            if first == 0:
                sums[t] = []
            cols = slice(first * CHUNK, end * CHUNK)
            part = norms.tile([P, 1], F32, name="sum_%d" % len(sums[t]))
            sums[t].append(part)
            if engine == "scalar":
                unused = squares.tile([P, ROW // 2], BF16, name="unused")
                nc.scalar.activation(
                    out=unused[:, : (end - first) * CHUNK],
                    in_=xw[t][:, cols],
                    func=ACT.Square,
                    accum_out=part[:],
                )
            else:
                unused = squares.tile([P, CHUNK], BF16, name="unused_v")
                nc.vector.scalar_tensor_tensor(
                    out=unused[:], in0=xw[t][:, cols], scalar=1.0, in1=xw[t][:, cols], op0=ALU.mult, op1=ALU.mult,
                    accum_out=part[:],
                )

        def root(t):
            total = totals.tile([P, 1], F32, name="total")
            for k, part in enumerate(sums[t]):
                nc.tensor.matmul(
                    out=total[:],
                    lhsT=same_node[:].rearrange("p n j -> p (n j)"),
                    rhs=part[:],
                    start=(k == 0),
                    stop=(k == len(sums[t]) - 1),
                )
            raised[t] = total

        def rectify(t):
            above = norms.tile([P, 1], F32, name="above")
            nc.scalar.activation(out=above[:], in_=raised[t][:], func=ACT.Relu, bias=minus_floor[:])
            raised[t] = above

        def invert(t):
            inverse[t] = norms.tile([P, 1], F32, name="inverse")
            nc.scalar.activation(out=inverse[t][:], in_=raised[t][:], func=ACT.Abs_reciprocal_sqrt, bias=floor[:])

        def normaliser(t, r):
            if t == SLABS - 1:
                return "vector"
            if t == SLABS - 2 and r >= 2:
                return "vector"
            return "gpsimd"

        def normalise(t, first=0, end=CHUNKS):
            if first == 0:
                xn[t] = normed.tile([P, ROW], BF16, name="xn_slab")
            for r in range(first, end):
                cols = slice(r * CHUNK, (r + 1) * CHUNK)
                how = normaliser(t, r)
                if how == "gpsimd":
                    if r % 2 == 1:
                        continue
                    stop = (r + 2) * CHUNK
                    if stop == ROW:
                        stop -= SHARE
                    cols = slice(r * CHUNK, stop)
                if how == "vector":
                    nc.vector.tensor_scalar(
                        out=xn[t][:, cols], in0=xw[t][:, cols], scalar1=inverse[t][:, 0:1], scalar2=None, op0=ALU.mult
                    )
                elif how == "scalar":
                    nc.scalar.activation(
                        out=xn[t][:, cols], in_=xw[t][:, cols], func=ACT.Copy, scale=inverse[t][:, 0:1]
                    )
                else:
                    nc.gpsimd.tensor_scalar(
                        out=xn[t][:, cols],
                        in0=xw[t][:, cols],
                        scalar1=inverse[t][:, 0:1],
                        scalar2=0.0,
                        op0=ALU.mult,
                        op1=ALU.add,
                    )

        def on_vector(t, r):
            return r == 3 and t < SLABS - 2

        def scalar_share(t):
            if SHARE:
                nc.scalar.activation(
                    out=xn[t][:, ROW - SHARE :], in_=xw[t][:, ROW - SHARE :], func=ACT.Copy, scale=inverse[t][:, 0:1]
                )

        def turn(t, r):
            b, g = place(t)
            if t % GROUPS == 0:
                grouped[b, r] = grouped_pool.tile([P, PASSES, GROUPS, PAIR], F32, name="grouped_chunk", align_bytes=64)
            words = xn[t][:].bitcast(F32)
            turned = turned_pool.tile([P, BLOCKS, P], F32, name="turned")
            for s in range(BLOCKS):
                c0 = r * WORDS + s * P
                nc.tensor.transpose(turned[:, s, :], words[:, c0 : c0 + P], pairing[:].rearrange("p h n j -> p (h n j)"))
            source = turned[:].rearrange("p s (h q) -> p (s h) q", h=2)
            if on_vector(t, r):
                nc.vector.tensor_copy(out=grouped[b, r][:, :, g, :], in_=source)
            else:
                nc.scalar.copy(out=grouped[b, r][:, :, g, :], in_=source)

        def quantise(b, r, first=0, end=PASSES):
            if first == 0:
                codes[b, r] = packed.tile([P, PASSES * NODES], U32, name="codes", align_bytes=64)
                scales[b, r] = packed.tile([P, PASSES * NODES], U8, name="scales", align_bytes=64)
            cols = slice(first * NODES, end * NODES)
            nc.vector.quantize_mx(
                out=codes[b, r][:, cols].bitcast(FP8X4),
                scales=scales[b, r][:, cols],
                in_=grouped[b, r][:, first:end].rearrange("p a g q -> p (a g q)").bitcast(BF16),
            )

        def accumulate(b, r, first=0, end=PASSES):
            if r == 0 and first == 0:
                if b == BATCH - 1:
                    gram[b] = w_bank_pool.tile([P, WORDS], F32, name="w_bank")
                else:
                    gram[b] = gram_pool.tile([P, WORDS], F32, name="gram_b")
            for s in range(first, end):
                nodes = slice(s * NODES, (s + 1) * NODES)
                nc.tensor.matmul_mx(
                    out=gram[b][:, :NODES],
                    lhsT=codes[b, r][:, nodes].bitcast(FP8X4),
                    lhsT_scale=scales[b, r][:, nodes],
                    rhs=codes[b, r][:, nodes].bitcast(FP8X4),
                    rhs_scale=scales[b, r][:, nodes],
                    start=(r == 0 and s == 0),
                    stop=(r == CHUNKS - 1 and s == PASSES - 1),
                )

        def fetch(b):
            cosines[b] = result.tile([P, NODES], F32, name="cos")
            nc.scalar.copy(out=cosines[b][:], in_=gram[b][:, :NODES])

        def threshold_and_store(b):
            cos = cosines[b]
            kept = result.tile([P, NODES], F32, name="kept")
            nc.vector.scalar_tensor_tensor(
                out=kept[:], in0=cos[:], scalar=EMP, in1=cos[:], op0=ALU.is_gt, op1=ALU.mult
            )
            final = result.tile([P, NODES], F32, name="final")
            nc.vector.tensor_scalar_max(out=final[:], in0=kept[:], scalar1=ZERO)
            nc.sync.dma_start(out=out[b], in_=final[:])

        one = const.tile([P, 1], F32)
        nc.vector.memset(one[:], 1.0)
        warm = const.tile([P, 1], F32)
        nc.scalar.activation(out=warm[:], in_=one[:], func=ACT.Abs_reciprocal_sqrt)
        floor = const.tile([P, 1], F32)
        nc.vector.tensor_scalar(out=floor[:], in0=one[:], scalar1=EPS * EPS, scalar2=None, op0=ALU.mult)
        minus_floor = const.tile([P, 1], F32)
        nc.vector.tensor_scalar(out=minus_floor[:], in0=one[:], scalar1=-EPS * EPS, scalar2=None, op0=ALU.mult)
        identity = const.tile([P, P], F32)
        masks.make_identity(nc, identity[:])
        pairing = const.tile([P, 2, GROUP_NODES, 2], F32)
        nc.vector.tensor_copy(out=pairing[:], in_=identity[:].rearrange("p (n h j) -> p h n j", h=2, j=2))
        node_of = const.tile([P, GROUP_NODES], F32)
        nc.vector.tensor_reduce(
            out=node_of[:],
            in_=identity[:].rearrange("p (n j) -> p n j", j=PACK),
            axis=AXIS.X,
            op=ALU.add,
        )
        same_node = const.tile([P, GROUP_NODES, PACK], F32)
        nc.vector.tensor_copy(
            out=same_node[:], in_=node_of[:].unsqueeze(2).to_broadcast([P, GROUP_NODES, PACK])
        )

        with tc.manual_schedule():
            load(0)
            load(1)
            for t in range(SLABS):
                if t + 2 < SLABS:
                    load(t + 2)
                lag = t - 2
                b, due = divmod(lag, GROUPS)
                fresh = t + 1 < GROUPS
                final = t == SLABS - 1
                if not fresh or t >= 1:
                    spread_w(t * CHUNKS + 2)
                if t == 1:
                    root(0)
                if lag >= 0:
                    turn(lag, 0)
                if lag >= 2 * GROUPS and due == 0:
                    fetch(b - 2)
                multiply(t, 0)
                if lag >= 0:
                    turn(lag, 1)
                if t >= 2:
                    root(t - 1)
                if not fresh or t >= 1:
                    spread_w(t * CHUNKS + 3)
                multiply(t, 1)
                if lag >= GROUPS:
                    quantise(b - 1, due)
                if lag >= 2 * GROUPS and due == 0:
                    threshold_and_store(b - 2)
                if t >= 1:
                    rectify(t - 1)
                if t >= 2:
                    scalar_share(t - 2)
                if t >= 1:
                    invert(t - 1)
                    normalise(t - 1, 0, CHUNKS if not final else 2)
                if t == 0:
                    square(t, 0, 1)
                    square(t, 1, 2)
                else:
                    square(t, 0, 2)
                multiply(t, 2)
                if not fresh:
                    spread_w(t * CHUNKS + 4)
                multiply(t, 3)
                if lag >= 0 and not final:
                    turn(lag, 2)
                if 0 <= t - GROUPS + 1 < CHUNKS:
                    turn_w(0, t - GROUPS + 1, "vector", False)
                if lag >= 0 and not final:
                    turn(lag, 3)
                if not fresh:
                    spread_w(t * CHUNKS + 5)
                if lag >= GROUPS and not final:
                    accumulate(b - 1, due)
                if not final:
                    square(t, 2, 4)
                if t == 0:
                    turn_w(1, 0, "vector", True)
                    turn_w(1, 1, "vector", False)
                    turn_w(1, 2, "vector", False)
                    spread_w(4)
                    spread_w(5)
                    turn_w(1, 3, "scalar", False)
                elif fresh:
                    turn_w(t + 1, 0, "vector", False)
                    turn_w(t + 1, 1, "vector", True)
                    turn_w(t + 1, 2, "vector", False)
                    spread_w(t * CHUNKS + 4)
                    spread_w(t * CHUNKS + 5)
                    turn_w(t + 1, 3, "scalar", False)
            last = SLABS - 1
            square(last, 2, 3)
            square(last, 3, 4)
            normalise(last - 1, 2)
            turn(last - 2, 2)
            turn(last - 2, 3)
            accumulate(BATCH - 2, 1)
            turn(last - 1, 0)
            quantise(BATCH - 2, 2)
            root(last)
            rectify(last)
            invert(last)
            normalise(last)
            turn(last - 1, 1)
            quantise(BATCH - 2, 3)
            turn(last - 1, 2)
            turn(last - 1, 3)
            for r in range(CHUNKS):
                turn(last, r)
            accumulate(BATCH - 2, 2)
            accumulate(BATCH - 2, 3)
            fetch(BATCH - 2)
            for r in range(CHUNKS):
                pieces = 2 if r == CHUNKS - 1 else 1
                for k in range(pieces):
                    span = (k * PASSES // pieces, (k + 1) * PASSES // pieces)
                    quantise(BATCH - 1, r, *span)
                    accumulate(BATCH - 1, r, *span)
            threshold_and_store(BATCH - 2)
            fetch(BATCH - 1)
            threshold_and_store(BATCH - 1)
